import numpy as np
import ml_dtypes


def mxq(x, axis, fmt="e4m3"):
    dtype, down = {"e4m3": (ml_dtypes.float8_e4m3fn, 7), "e5m2": (ml_dtypes.float8_e5m2, 14)}[fmt]
    v = np.moveaxis(np.asarray(x, np.float32).astype(ml_dtypes.bfloat16).astype(np.float64), axis, -1)
    blocks = v.reshape(v.shape[:-1] + (-1, 32))
    amax = np.abs(blocks).max(-1, keepdims=True)
    byte = np.maximum(np.where(amax > 0, np.frexp(amax)[1] - 1 + 127, 0) - down, 1)
    scale = np.exp2(byte - 127.0)
    codes = (blocks / scale).astype(np.float32).astype(dtype).astype(np.float64)
    return np.moveaxis((codes * scale).reshape(v.shape), -1, axis)


WIDE = False


def mx_kscale(k):
    if not WIDE:
        return np.ones(k)
    levels = np.array([20, -20, 10, -10, 0])
    a = np.random.permutation(np.resize(levels, k // 512 * 4)).reshape(k // 512, 4)
    idx = np.arange(k)
    return np.exp2(a[idx // 512, idx % 128 // 32])


BF16 = ml_dtypes.bfloat16


def bf(x):
    return np.asarray(x, np.float32).astype(BF16)


def f64(x):
    return np.asarray(x).astype(np.float64)


N, C, F, H, W, KH, KW = 8192, 80, 64, 4, 4, 3, 3
P = H * W


def setup_inputs():
    s = mx_kscale(N)[:, None, None, None]
    x = np.random.standard_normal((N, C, H, W)) * 2.0 * s
    k = np.random.standard_normal((F, C, H, W)) * 2.0 / np.sqrt(C)
    g = np.random.standard_normal((N, F, H, W)) * np.exp2(np.random.randint(-12, 1, (N, 1, 1, 1))) / s
    return {"x_dct": bf(x), "k_dct": bf(k), "grad_out": bf(g)}


def reference(x_dct, k_dct, grad_out):
    xq = mxq(f64(x_dct), 0, "e4m3").reshape(N, C, P).transpose(2, 0, 1)
    gq = mxq(f64(grad_out), 0, "e5m2").reshape(N, F, P).transpose(2, 1, 0)
    r = gq @ xq
    return r.transpose(1, 2, 0).reshape(F, C, H, W)

@@ -1,0 +1,154 @@
+from contextlib import ExitStack
+
+import concourse.mybir as mybir
+
+BF16 = mybir.dt.bfloat16
+F32 = mybir.dt.float32
+U32 = mybir.dt.uint32
+U8 = mybir.dt.uint8
+E4M3_X4 = mybir.dt.float8_e4m3fn_x4
+E5M2_X4 = mybir.dt.float8_e5m2_x4
+
+IMAGES, CHANNELS, FILTERS = 8192, 80, 64
+P = 128
+PACK = 4
+K_PASS = P * PACK
+PASSES = IMAGES // K_PASS
+UPPER = 2
+HALVES = 2
+RUN = 4
+BANKS = HALVES * RUN
+
+G_PAIR = UPPER * FILTERS
+X_PAIR = UPPER * CHANNELS
+G_COLS = RUN * G_PAIR
+X_COLS = RUN * X_PAIR
+N_MOVING = 512
+SCALE_ALIGN = 64
+X_QUANT_WIDE = 2048
+
+RAW_BUFS = 4
+UNIT_BUFS = 3
+
+FLOPS = 2 * 16 * FILTERS * CHANNELS * IMAGES
+BYTES = 2 * IMAGES * 16 * (CHANNELS + FILTERS) + 4 * 16 * FILTERS * CHANNELS
+
+
+def window_start(i):
+    return min(i * X_PAIR // SCALE_ALIGN * SCALE_ALIGN, X_COLS - N_MOVING)
+
+
+def tile_convdct_pa_k_kernel(tc, x_dct, k_dct, grad_out, out):
+    nc = tc.nc
+    with ExitStack() as ctx:
+        ctx.enter_context(tc.manual_schedule())
+        raw = ctx.enter_context(tc.tile_pool(name="raw", bufs=RAW_BUFS))
+        grouped = ctx.enter_context(tc.tile_pool(name="grouped", bufs=UNIT_BUFS))
+        quantised = ctx.enter_context(tc.tile_pool(name="quantised", bufs=UNIT_BUFS))
+        results = ctx.enter_context(tc.tile_pool(name="results", bufs=1))
+        psum = ctx.enter_context(tc.psum_pool(name="psum", bufs=1))
+
+        banks = [psum.tile([P, N_MOVING], F32, name="bank%d" % j) for j in range(BANKS)]
+
+        def load_pass(s):
+            rows = slice(s * K_PASS, (s + 1) * K_PASS)
+            x_raw = raw.tile([P, PACK, CHANNELS, UPPER, HALVES, RUN], BF16, name="x_raw")
+            nc.sync.dma_start(
+                out=x_raw[:].rearrange("p t c a h i -> p (t c a h i)"),
+                in_=x_dct[rows].rearrange("(p t) c h w -> p (t c h w)", t=PACK),
+            )
+            g_raw = raw.tile([P, PACK, FILTERS, UPPER, HALVES, RUN], BF16, name="g_raw")
+            nc.sync.dma_start(
+                out=g_raw[:].rearrange("p t f a h i -> p (t f a h i)"),
+                in_=grad_out[rows].rearrange("(p t) f h w -> p (t f h w)", t=PACK),
+            )
+            return x_raw, g_raw
+
+        def regroup(x_raw, g_raw, h):
+            g_grp = grouped.tile([P, RUN, UPPER, FILTERS, PACK], BF16, name="g_grp", align_bytes=64)
+            nc.vector.tensor_copy(
+                out=g_grp[:].rearrange("p i a f t -> p a f t i"),
+                in_=g_raw[:, :, :, :, h, :].rearrange("p t f a i -> p a f t i"),
+            )
+            x_grp = grouped.tile([P, RUN, UPPER, CHANNELS, PACK], BF16, name="x_grp", align_bytes=64)
+            for a in range(UPPER):
+                nc.scalar.copy(
+                    out=x_grp[:, :, a, :, :].rearrange("p i c t -> p c t i"),
+                    in_=x_raw[:, :, :, a, h, :].rearrange("p t c i -> p c t i"),
+                )
+            return x_grp, g_grp
+
+        def quantise_and_multiply(x_grp, g_grp, s, h):
+            g_codes = quantised.tile([P, G_COLS], U32, name="g_codes", align_bytes=64)
+            g_scales = quantised.tile([P, G_COLS], U8, name="g_scales", align_bytes=64)
+            nc.vector.quantize_mx(
+                out=g_codes[:].bitcast(E5M2_X4),
+                scales=g_scales[:],
+                in_=g_grp[:].rearrange("p i a f t -> p (i a f t)"),
+            )
+            x_codes = quantised.tile([P, X_COLS], U32, name="x_codes", align_bytes=64)
+            x_scales = quantised.tile([P, X_COLS], U8, name="x_scales", align_bytes=64)
+            x_flat = x_grp[:].rearrange("p i a c t -> p (i a c t)")
+            wide = X_QUANT_WIDE // PACK
+            for first, last in ((0, wide), (wide, X_COLS)):
+                nc.vector.quantize_mx(
+                    out=x_codes[:, first:last].bitcast(E4M3_X4),
+                    scales=x_scales[:, first:last],
+                    in_=x_flat[:, first * PACK : last * PACK],
+                )
+            for i in range(RUN):
+                pair = slice(i * G_PAIR, (i + 1) * G_PAIR)
+                window = slice(window_start(i), window_start(i) + N_MOVING)
+                nc.tensor.matmul_mx(
+                    out=banks[h * RUN + i][:],
+                    lhsT=g_codes[:, pair].bitcast(E5M2_X4),
+                    lhsT_scale=g_scales[:, pair],
+                    rhs=x_codes[:, window].bitcast(E4M3_X4),
+                    rhs_scale=x_scales[:, window],
+                    start=(s == 0),
+                    stop=(s == PASSES - 1),
+                )
+
+        picked = results.tile([P, BANKS, CHANNELS], F32, name="picked")
+        result = results.tile([P, CHANNELS, BANKS], F32, name="result")
+
+        def pick(j, copy_lower, copy_upper):
+            first = (j % RUN) * X_PAIR - window_start(j % RUN)
+            copy_lower(
+                out=picked[0:FILTERS, j, :],
+                in_=banks[j][0:FILTERS, first : first + CHANNELS],
+            )
+            copy_upper(
+                out=picked[FILTERS:P, j, :],
+                in_=banks[j][FILTERS:P, first + CHANNELS : first + X_PAIR],
+            )
+
+        def reorder(h):
+            js = slice(h * RUN, (h + 1) * RUN)
+            nc.vector.tensor_copy(
+                out=result[:, :, js], in_=picked[:, js, :].rearrange("p j c -> p c j")
+            )
+
+        loaded = [load_pass(s) for s in range(RAW_BUFS)]
+        waiting = None
+        for s in range(PASSES):
+            x_raw, g_raw = loaded[s]
+            for h in range(HALVES):
+                x_grp, g_grp = regroup(x_raw, g_raw, h)
+                if waiting is not None:
+                    quantise_and_multiply(*waiting)
+                waiting = (x_grp, g_grp, s, h)
+            if s + RAW_BUFS < PASSES:
+                loaded.append(load_pass(s + RAW_BUFS))
+
+        for j in range(RUN):
+            pick(j, nc.scalar.copy, nc.scalar.copy)
+        quantise_and_multiply(*waiting)
+        reorder(0)
+        for j in range(RUN, BANKS):
+            pick(j, nc.vector.tensor_copy, nc.scalar.copy)
+        reorder(1)
+
+        out_halves = out.rearrange("f c (a h) w -> a f c (h w)", a=UPPER)
+        nc.sync.dma_start(out=out_halves[0], in_=result[0:FILTERS])
+        nc.scalar.dma_start(out=out_halves[1], in_=result[FILTERS:P])

@@ -1,6 +1,7 @@
 from contextlib import ExitStack
 
 import concourse.mybir as mybir
+from concourse.masks import make_identity
 
 BF16 = mybir.dt.bfloat16
 F32 = mybir.dt.float32
@@ -14,18 +15,23 @@ P = 128
 PACK = 4
 K_PASS = P * PACK
 PASSES = IMAGES // K_PASS
-UPPER = 2
-HALVES = 2
-RUN = 4
-BANKS = HALVES * RUN
+UNITS = 2
+ROWS = 2
+W = 4
+PAIRS = W // 2
+UNIT_BANKS = ROWS * PAIRS
+BANKS = UNITS * UNIT_BANKS
 
-G_PAIR = UPPER * FILTERS
-X_PAIR = UPPER * CHANNELS
-G_COLS = RUN * G_PAIR
-X_COLS = RUN * X_PAIR
+G_PAIR = 2 * FILTERS
+X_ROW = CHANNELS * W
+G_COLS = ROWS * W * FILTERS
+X_COLS = ROWS * X_ROW
 N_MOVING = 512
 SCALE_ALIGN = 64
 X_QUANT_WIDE = 2048
+HALF_CHANNELS = CHANNELS // 2
+
+X_ON_VECTOR = 4
 
 RAW_BUFS = 4
 UNIT_BUFS = 3
@@ -34,61 +40,66 @@ FLOPS = 2 * 16 * FILTERS * CHANNELS * IMAGES
 BYTES = 2 * IMAGES * 16 * (CHANNELS + FILTERS) + 4 * 16 * FILTERS * CHANNELS
 
 
-def window_start(i):
-    return min(i * X_PAIR // SCALE_ALIGN * SCALE_ALIGN, X_COLS - N_MOVING)
+def window_start(r):
+    return min(r * X_ROW // SCALE_ALIGN * SCALE_ALIGN, X_COLS - N_MOVING)
 
 
 def tile_convdct_pa_k_kernel(tc, x_dct, k_dct, grad_out, out):
     nc = tc.nc
     with ExitStack() as ctx:
         ctx.enter_context(tc.manual_schedule())
+        consts = ctx.enter_context(tc.tile_pool(name="consts", bufs=1))
         raw = ctx.enter_context(tc.tile_pool(name="raw", bufs=RAW_BUFS))
         grouped = ctx.enter_context(tc.tile_pool(name="grouped", bufs=UNIT_BUFS))
         quantised = ctx.enter_context(tc.tile_pool(name="quantised", bufs=UNIT_BUFS))
         results = ctx.enter_context(tc.tile_pool(name="results", bufs=1))
         psum = ctx.enter_context(tc.psum_pool(name="psum", bufs=1))
 
-        banks = [psum.tile([P, N_MOVING], F32, name="bank%d" % j) for j in range(BANKS)]
+        banks = [psum.tile([P, N_MOVING], F32, name="bank%d" % b) for b in range(BANKS)]
 
         def load_pass(s):
             rows = slice(s * K_PASS, (s + 1) * K_PASS)
-            x_raw = raw.tile([P, PACK, CHANNELS, UPPER, HALVES, RUN], BF16, name="x_raw")
+            x_raw = raw.tile([P, PACK, CHANNELS, UNITS, ROWS, W], BF16, name="x_raw")
             nc.sync.dma_start(
-                out=x_raw[:].rearrange("p t c a h i -> p (t c a h i)"),
+                out=x_raw[:].rearrange("p t c u r w -> p (t c u r w)"),
                 in_=x_dct[rows].rearrange("(p t) c h w -> p (t c h w)", t=PACK),
             )
-            g_raw = raw.tile([P, PACK, FILTERS, UPPER, HALVES, RUN], BF16, name="g_raw")
+            g_raw = raw.tile([P, PACK, FILTERS, UNITS, ROWS, W], BF16, name="g_raw")
             nc.sync.dma_start(
-                out=g_raw[:].rearrange("p t f a h i -> p (t f a h i)"),
+                out=g_raw[:].rearrange("p t f u r w -> p (t f u r w)"),
                 in_=grad_out[rows].rearrange("(p t) f h w -> p (t f h w)", t=PACK),
             )
             return x_raw, g_raw
 
-        def regroup(x_raw, g_raw, h):
-            g_grp = grouped.tile([P, RUN, UPPER, FILTERS, PACK], BF16, name="g_grp", align_bytes=64)
+        def regroup(x_raw, g_raw, u):
+            g_grp = grouped.tile([P, ROWS, W, FILTERS, PACK], BF16, name="g_grp", align_bytes=64)
             nc.vector.tensor_copy(
-                out=g_grp[:].rearrange("p i a f t -> p a f t i"),
-                in_=g_raw[:, :, :, :, h, :].rearrange("p t f a i -> p a f t i"),
+                out=g_grp[:].rearrange("p r w f t -> p r f t w"),
+                in_=g_raw[:, :, :, u, :, :].rearrange("p t f r w -> p r f t w"),
             )
-            x_grp = grouped.tile([P, RUN, UPPER, CHANNELS, PACK], BF16, name="x_grp", align_bytes=64)
-            for a in range(UPPER):
+            x_grp = grouped.tile([P, ROWS, CHANNELS, W, PACK], BF16, name="x_grp", align_bytes=64)
+            nc.vector.tensor_copy(
+                out=x_grp[:, :, 0:X_ON_VECTOR, :, :].rearrange("p r c w t -> p r c t w"),
+                in_=x_raw[:, :, 0:X_ON_VECTOR, u, :, :].rearrange("p t c r w -> p r c t w"),
+            )
+            for r in range(ROWS):
                 nc.scalar.copy(
-                    out=x_grp[:, :, a, :, :].rearrange("p i c t -> p c t i"),
-                    in_=x_raw[:, :, :, a, h, :].rearrange("p t c i -> p c t i"),
+                    out=x_grp[:, r, X_ON_VECTOR:, :, :].rearrange("p c w t -> p c t w"),
+                    in_=x_raw[:, :, X_ON_VECTOR:, u, r, :].rearrange("p t c w -> p c t w"),
                 )
             return x_grp, g_grp
 
-        def quantise_and_multiply(x_grp, g_grp, s, h):
+        def quantise_and_multiply(x_grp, g_grp, s, u):
             g_codes = quantised.tile([P, G_COLS], U32, name="g_codes", align_bytes=64)
             g_scales = quantised.tile([P, G_COLS], U8, name="g_scales", align_bytes=64)
             nc.vector.quantize_mx(
                 out=g_codes[:].bitcast(E5M2_X4),
                 scales=g_scales[:],
-                in_=g_grp[:].rearrange("p i a f t -> p (i a f t)"),
+                in_=g_grp[:].rearrange("p r w f t -> p (r w f t)"),
             )
             x_codes = quantised.tile([P, X_COLS], U32, name="x_codes", align_bytes=64)
             x_scales = quantised.tile([P, X_COLS], U8, name="x_scales", align_bytes=64)
-            x_flat = x_grp[:].rearrange("p i a c t -> p (i a c t)")
+            x_flat = x_grp[:].rearrange("p r c w t -> p (r c w t)")
             wide = X_QUANT_WIDE // PACK
             for first, last in ((0, wide), (wide, X_COLS)):
                 nc.vector.quantize_mx(
@@ -96,59 +107,86 @@ def tile_convdct_pa_k_kernel(tc, x_dct, k_dct, grad_out, out):
                     scales=x_scales[:, first:last],
                     in_=x_flat[:, first * PACK : last * PACK],
                 )
-            for i in range(RUN):
-                pair = slice(i * G_PAIR, (i + 1) * G_PAIR)
-                window = slice(window_start(i), window_start(i) + N_MOVING)
-                nc.tensor.matmul_mx(
-                    out=banks[h * RUN + i][:],
-                    lhsT=g_codes[:, pair].bitcast(E5M2_X4),
-                    lhsT_scale=g_scales[:, pair],
-                    rhs=x_codes[:, window].bitcast(E4M3_X4),
-                    rhs_scale=x_scales[:, window],
-                    start=(s == 0),
-                    stop=(s == PASSES - 1),
+            for r in range(ROWS):
+                window = slice(window_start(r), window_start(r) + N_MOVING)
+                for q in range(PAIRS):
+                    pair = slice((r * PAIRS + q) * G_PAIR, (r * PAIRS + q + 1) * G_PAIR)
+                    nc.tensor.matmul_mx(
+                        out=banks[u * UNIT_BANKS + r * PAIRS + q][:],
+                        lhsT=g_codes[:, pair].bitcast(E5M2_X4),
+                        lhsT_scale=g_scales[:, pair],
+                        rhs=x_codes[:, window].bitcast(E4M3_X4),
+                        rhs_scale=x_scales[:, window],
+                        start=(s == 0),
+                        stop=(s == PASSES - 1),
+                    )
+
+        identity = consts.tile([P, P], F32, name="identity")
+        make_identity(nc, identity[:])
+        swap = consts.tile([P, P], F32, name="swap")
+        nc.vector.tensor_copy(out=swap[:, 0:FILTERS], in_=identity[:, FILTERS:P])
+        nc.vector.tensor_copy(out=swap[:, FILTERS:P], in_=identity[:, 0:FILTERS])
+
+        own = results.tile([P, BANKS, CHANNELS], F32, name="own")
+        final = results.tile([P, HALF_CHANNELS, BANKS, 2], F32, name="final")
+        halves = (slice(0, FILTERS), slice(FILTERS, P))
+
+        def pick_and_swap(u, copies):
+            for b in range(UNIT_BANKS):
+                r, q = divmod(b, PAIRS)
+                first = r * X_ROW - window_start(r)
+                for e in range(2):
+                    row = banks[u * UNIT_BANKS + b][halves[e], first : first + X_ROW]
+                    copies[e](
+                        out=own[halves[e], u * UNIT_BANKS + b, :],
+                        in_=row.rearrange("p (c w) -> p c w", w=W)[:, :, 2 * q + e],
+                    )
+            other = psum.tile([P, UNIT_BANKS, CHANNELS], F32, name="other", tag="bank%d" % u)
+            for b in range(UNIT_BANKS):
+                nc.tensor.matmul(
+                    out=other[:, b, :],
+                    lhsT=swap[:],
+                    rhs=own[:, u * UNIT_BANKS + b, :],
+                    start=True,
+                    stop=True,
                 )
+            return other
 
-        picked = results.tile([P, BANKS, CHANNELS], F32, name="picked")
-        result = results.tile([P, CHANNELS, BANKS], F32, name="result")
-
-        def pick(j, copy_lower, copy_upper):
-            first = (j % RUN) * X_PAIR - window_start(j % RUN)
-            copy_lower(
-                out=picked[0:FILTERS, j, :],
-                in_=banks[j][0:FILTERS, first : first + CHANNELS],
-            )
-            copy_upper(
-                out=picked[FILTERS:P, j, :],
-                in_=banks[j][FILTERS:P, first + CHANNELS : first + X_PAIR],
-            )
-
-        def reorder(h):
-            js = slice(h * RUN, (h + 1) * RUN)
-            nc.vector.tensor_copy(
-                out=result[:, :, js], in_=picked[:, js, :].rearrange("p j c -> p c j")
-            )
+        def assemble(u, other, copies):
+            unit = slice(u * UNIT_BANKS, (u + 1) * UNIT_BANKS)
+            for d in range(2):
+                mine = slice(d * HALF_CHANNELS, (d + 1) * HALF_CHANNELS)
+                copies[d](
+                    out=final[halves[d], :, unit, d],
+                    in_=own[halves[d], unit, mine].rearrange("p b c -> p c b"),
+                )
+            for d in range(2):
+                mine = slice(d * HALF_CHANNELS, (d + 1) * HALF_CHANNELS)
+                copies[d](
+                    out=final[halves[d], :, unit, 1 - d],
+                    in_=other[halves[d], :, mine].rearrange("p b c -> p c b"),
+                )
 
         loaded = [load_pass(s) for s in range(RAW_BUFS)]
         waiting = None
         for s in range(PASSES):
             x_raw, g_raw = loaded[s]
-            for h in range(HALVES):
-                x_grp, g_grp = regroup(x_raw, g_raw, h)
+            for u in range(UNITS):
+                x_grp, g_grp = regroup(x_raw, g_raw, u)
                 if waiting is not None:
                     quantise_and_multiply(*waiting)
-                waiting = (x_grp, g_grp, s, h)
+                waiting = (x_grp, g_grp, s, u)
             if s + RAW_BUFS < PASSES:
                 loaded.append(load_pass(s + RAW_BUFS))
 
-        for j in range(RUN):
-            pick(j, nc.scalar.copy, nc.scalar.copy)
+        both = (nc.vector.tensor_copy, nc.scalar.copy)
+        other_0 = pick_and_swap(0, (nc.scalar.copy, nc.scalar.copy))
         quantise_and_multiply(*waiting)
-        reorder(0)
-        for j in range(RUN, BANKS):
-            pick(j, nc.vector.tensor_copy, nc.scalar.copy)
-        reorder(1)
+        assemble(0, other_0, both)
+        other_1 = pick_and_swap(1, both)
+        assemble(1, other_1, both)
 
-        out_halves = out.rearrange("f c (a h) w -> a f c (h w)", a=UPPER)
-        nc.sync.dma_start(out=out_halves[0], in_=result[0:FILTERS])
-        nc.scalar.dma_start(out=out_halves[1], in_=result[FILTERS:P])
+        out_halves = out.rearrange("f (d c) h w -> d f (c h w)", d=2)
+        final_flat = final[:].rearrange("p c b e -> p (c b e)")
+        nc.sync.dma_start(out=out_halves[0], in_=final_flat[halves[0]])
+        nc.scalar.dma_start(out=out_halves[1], in_=final_flat[halves[1]])

@@ -79,14 +79,13 @@ def tile_convdct_pa_k_kernel(tc, x_dct, k_dct, grad_out, out):
             )
             x_grp = grouped.tile([P, ROWS, CHANNELS, W, PACK], BF16, name="x_grp", align_bytes=64)
             nc.vector.tensor_copy(
-                out=x_grp[:, :, 0:X_ON_VECTOR, :, :].rearrange("p r c w t -> p r c t w"),
-                in_=x_raw[:, :, 0:X_ON_VECTOR, u, :, :].rearrange("p t c r w -> p r c t w"),
+                out=x_grp[:, :, 0:X_ON_VECTOR, :, :].rearrange("p r c w t -> p c t r w"),
+                in_=x_raw[:, :, 0:X_ON_VECTOR, u, :, :].rearrange("p t c r w -> p c t r w"),
             )
-            for r in range(ROWS):
-                nc.scalar.copy(
-                    out=x_grp[:, r, X_ON_VECTOR:, :, :].rearrange("p c w t -> p c t w"),
-                    in_=x_raw[:, :, X_ON_VECTOR:, u, r, :].rearrange("p t c w -> p c t w"),
-                )
+            nc.scalar.copy(
+                out=x_grp[:, :, X_ON_VECTOR:, :, :].rearrange("p r c w t -> p c t r w"),
+                in_=x_raw[:, :, X_ON_VECTOR:, u, :, :].rearrange("p t c r w -> p c t r w"),
+            )
             return x_grp, g_grp
 
         def quantise_and_multiply(x_grp, g_grp, s, u):

@@ -15,33 +15,44 @@ P = 128
 PACK = 4
 K_PASS = P * PACK
 PASSES = IMAGES // K_PASS
-UNITS = 2
-ROWS = 2
+H = 4
 W = 4
 PAIRS = W // 2
-UNIT_BANKS = ROWS * PAIRS
-BANKS = UNITS * UNIT_BANKS
+BANKS = H * PAIRS
 
 G_PAIR = 2 * FILTERS
-X_ROW = CHANNELS * W
-G_COLS = ROWS * W * FILTERS
-X_COLS = ROWS * X_ROW
+G_ROW = W * FILTERS
+X_ROW = W * CHANNELS
+G_COLS = H * G_ROW
+X_COLS = H * X_ROW
 N_MOVING = 512
-SCALE_ALIGN = 64
-X_QUANT_WIDE = 2048
+MAX_QUANT_COLS = 1024
 HALF_CHANNELS = CHANNELS // 2
 
 X_ON_VECTOR = 4
 
 RAW_BUFS = 4
-UNIT_BUFS = 3
+PASS_BUFS = 3
 
 FLOPS = 2 * 16 * FILTERS * CHANNELS * IMAGES
 BYTES = 2 * IMAGES * 16 * (CHANNELS + FILTERS) + 4 * 16 * FILTERS * CHANNELS
 
+UNITS = [(s, 0, H) for s in range(PASSES - 1)] + [(PASSES - 1, 0, 2), (PASSES - 1, 2, 3), (PASSES - 1, 3, 4)]
 
-def window_start(r):
-    return min(r * X_ROW // SCALE_ALIGN * SCALE_ALIGN, X_COLS - N_MOVING)
+
+def window_start(h):
+    return 0 if h == 0 else (h + 1) * X_ROW - N_MOVING
+
+
+def quantise_pieces(first, last):
+    pieces = []
+    while first < last:
+        width = MAX_QUANT_COLS
+        while width > last - first:
+            width //= 2
+        pieces.append((first, first + width))
+        first += width
+    return pieces
 
 
 def tile_convdct_pa_k_kernel(tc, x_dct, k_dct, grad_out, out):
@@ -50,8 +61,8 @@ def tile_convdct_pa_k_kernel(tc, x_dct, k_dct, grad_out, out):
         ctx.enter_context(tc.manual_schedule())
         consts = ctx.enter_context(tc.tile_pool(name="consts", bufs=1))
         raw = ctx.enter_context(tc.tile_pool(name="raw", bufs=RAW_BUFS))
-        grouped = ctx.enter_context(tc.tile_pool(name="grouped", bufs=UNIT_BUFS))
-        quantised = ctx.enter_context(tc.tile_pool(name="quantised", bufs=UNIT_BUFS))
+        grouped = ctx.enter_context(tc.tile_pool(name="grouped", bufs=PASS_BUFS))
+        quantised = ctx.enter_context(tc.tile_pool(name="quantised", bufs=PASS_BUFS))
         results = ctx.enter_context(tc.tile_pool(name="results", bufs=1))
         psum = ctx.enter_context(tc.psum_pool(name="psum", bufs=1))
 
@@ -59,63 +70,70 @@ def tile_convdct_pa_k_kernel(tc, x_dct, k_dct, grad_out, out):
 
         def load_pass(s):
             rows = slice(s * K_PASS, (s + 1) * K_PASS)
-            x_raw = raw.tile([P, PACK, CHANNELS, UNITS, ROWS, W], BF16, name="x_raw")
+            x_raw = raw.tile([P, PACK, CHANNELS, H, W], BF16, name="x_raw")
             nc.sync.dma_start(
-                out=x_raw[:].rearrange("p t c u r w -> p (t c u r w)"),
+                out=x_raw[:].rearrange("p t c h w -> p (t c h w)"),
                 in_=x_dct[rows].rearrange("(p t) c h w -> p (t c h w)", t=PACK),
             )
-            g_raw = raw.tile([P, PACK, FILTERS, UNITS, ROWS, W], BF16, name="g_raw")
+            g_raw = raw.tile([P, PACK, FILTERS, H, W], BF16, name="g_raw")
             nc.sync.dma_start(
-                out=g_raw[:].rearrange("p t f u r w -> p (t f u r w)"),
+                out=g_raw[:].rearrange("p t f h w -> p (t f h w)"),
                 in_=grad_out[rows].rearrange("(p t) f h w -> p (t f h w)", t=PACK),
             )
             return x_raw, g_raw
 
-        def regroup(x_raw, g_raw, u):
-            g_grp = grouped.tile([P, ROWS, W, FILTERS, PACK], BF16, name="g_grp", align_bytes=64)
-            nc.vector.tensor_copy(
-                out=g_grp[:].rearrange("p r w f t -> p r f t w"),
-                in_=g_raw[:, :, :, u, :, :].rearrange("p t f r w -> p r f t w"),
+        def pass_tiles():
+            return dict(
+                g_grp=grouped.tile([P, H, W, FILTERS, PACK], BF16, name="g_grp", align_bytes=64),
+                x_grp=grouped.tile([P, H, CHANNELS, W, PACK], BF16, name="x_grp", align_bytes=64),
+                g_codes=quantised.tile([P, G_COLS], U32, name="g_codes", align_bytes=64),
+                g_scales=quantised.tile([P, G_COLS], U8, name="g_scales", align_bytes=64),
+                x_codes=quantised.tile([P, X_COLS], U32, name="x_codes", align_bytes=64),
+                x_scales=quantised.tile([P, X_COLS], U8, name="x_scales", align_bytes=64),
             )
-            x_grp = grouped.tile([P, ROWS, CHANNELS, W, PACK], BF16, name="x_grp", align_bytes=64)
-            nc.vector.tensor_copy(
-                out=x_grp[:, :, 0:X_ON_VECTOR, :, :].rearrange("p r c w t -> p c t r w"),
-                in_=x_raw[:, :, 0:X_ON_VECTOR, u, :, :].rearrange("p t c r w -> p c t r w"),
-            )
-            nc.scalar.copy(
-                out=x_grp[:, :, X_ON_VECTOR:, :, :].rearrange("p r c w t -> p c t r w"),
-                in_=x_raw[:, :, X_ON_VECTOR:, u, :, :].rearrange("p t c r w -> p c t r w"),
-            )
-            return x_grp, g_grp
 
-        def quantise_and_multiply(x_grp, g_grp, s, u):
-            g_codes = quantised.tile([P, G_COLS], U32, name="g_codes", align_bytes=64)
-            g_scales = quantised.tile([P, G_COLS], U8, name="g_scales", align_bytes=64)
-            nc.vector.quantize_mx(
-                out=g_codes[:].bitcast(E5M2_X4),
-                scales=g_scales[:],
-                in_=g_grp[:].rearrange("p r w f t -> p (r w f t)"),
+        def regroup(x_raw, g_raw, tiles, h0, h1):
+            rows = slice(h0, h1)
+            nc.vector.tensor_copy(
+                out=tiles["g_grp"][:, rows, :, :, :].rearrange("p h w f t -> p h f t w"),
+                in_=g_raw[:, :, :, rows, :].rearrange("p t f h w -> p h f t w"),
             )
-            x_codes = quantised.tile([P, X_COLS], U32, name="x_codes", align_bytes=64)
-            x_scales = quantised.tile([P, X_COLS], U8, name="x_scales", align_bytes=64)
-            x_flat = x_grp[:].rearrange("p r c w t -> p (r c w t)")
-            wide = X_QUANT_WIDE // PACK
-            for first, last in ((0, wide), (wide, X_COLS)):
+            nc.vector.tensor_copy(
+                out=tiles["x_grp"][:, rows, 0:X_ON_VECTOR, :, :].rearrange("p h c w t -> p h c t w"),
+                in_=x_raw[:, :, 0:X_ON_VECTOR, rows, :].rearrange("p t c h w -> p h c t w"),
+            )
+            for first in range(h0, h1, 2):
+                two = slice(first, min(first + 2, h1))
+                nc.scalar.copy(
+                    out=tiles["x_grp"][:, two, X_ON_VECTOR:, :, :].rearrange("p h c w t -> p c t h w"),
+                    in_=x_raw[:, :, X_ON_VECTOR:, two, :].rearrange("p t c h w -> p c t h w"),
+                )
+
+        def quantise_and_multiply(tiles, s, h0, h1):
+            g_flat = tiles["g_grp"][:].rearrange("p h w f t -> p (h w f t)")
+            for first, last in quantise_pieces(h0 * G_ROW, h1 * G_ROW):
                 nc.vector.quantize_mx(
-                    out=x_codes[:, first:last].bitcast(E4M3_X4),
-                    scales=x_scales[:, first:last],
+                    out=tiles["g_codes"][:, first:last].bitcast(E5M2_X4),
+                    scales=tiles["g_scales"][:, first:last],
+                    in_=g_flat[:, first * PACK : last * PACK],
+                )
+            x_flat = tiles["x_grp"][:].rearrange("p h c w t -> p (h c w t)")
+            for first, last in quantise_pieces(h0 * X_ROW, h1 * X_ROW):
+                nc.vector.quantize_mx(
+                    out=tiles["x_codes"][:, first:last].bitcast(E4M3_X4),
+                    scales=tiles["x_scales"][:, first:last],
                     in_=x_flat[:, first * PACK : last * PACK],
                 )
-            for r in range(ROWS):
-                window = slice(window_start(r), window_start(r) + N_MOVING)
+            for h in range(h0, h1):
+                window = slice(window_start(h), window_start(h) + N_MOVING)
                 for q in range(PAIRS):
-                    pair = slice((r * PAIRS + q) * G_PAIR, (r * PAIRS + q + 1) * G_PAIR)
+                    pair = slice((h * PAIRS + q) * G_PAIR, (h * PAIRS + q + 1) * G_PAIR)
                     nc.tensor.matmul_mx(
-                        out=banks[u * UNIT_BANKS + r * PAIRS + q][:],
-                        lhsT=g_codes[:, pair].bitcast(E5M2_X4),
-                        lhsT_scale=g_scales[:, pair],
-                        rhs=x_codes[:, window].bitcast(E4M3_X4),
-                        rhs_scale=x_scales[:, window],
+                        out=banks[h * PAIRS + q][:],
+                        lhsT=tiles["g_codes"][:, pair].bitcast(E5M2_X4),
+                        lhsT_scale=tiles["g_scales"][:, pair],
+                        rhs=tiles["x_codes"][:, window].bitcast(E4M3_X4),
+                        rhs_scale=tiles["x_scales"][:, window],
                         start=(s == 0),
                         stop=(s == PASSES - 1),
                     )
@@ -130,60 +148,76 @@ def tile_convdct_pa_k_kernel(tc, x_dct, k_dct, grad_out, out):
         final = results.tile([P, HALF_CHANNELS, BANKS, 2], F32, name="final")
         halves = (slice(0, FILTERS), slice(FILTERS, P))
 
-        def pick_and_swap(u, copies):
-            for b in range(UNIT_BANKS):
-                r, q = divmod(b, PAIRS)
-                first = r * X_ROW - window_start(r)
-                for e in range(2):
-                    row = banks[u * UNIT_BANKS + b][halves[e], first : first + X_ROW]
+        def pick(h0, h1, copies):
+            for e in range(2):
+                for b in range(h0 * PAIRS, h1 * PAIRS):
+                    h, q = divmod(b, PAIRS)
+                    first = h * X_ROW - window_start(h)
+                    row = banks[b][halves[e], first : first + X_ROW]
                     copies[e](
-                        out=own[halves[e], u * UNIT_BANKS + b, :],
+                        out=own[halves[e], b, :],
                         in_=row.rearrange("p (c w) -> p c w", w=W)[:, :, 2 * q + e],
                     )
-            other = psum.tile([P, UNIT_BANKS, CHANNELS], F32, name="other", tag="bank%d" % u)
-            for b in range(UNIT_BANKS):
-                nc.tensor.matmul(
-                    out=other[:, b, :],
-                    lhsT=swap[:],
-                    rhs=own[:, u * UNIT_BANKS + b, :],
-                    start=True,
-                    stop=True,
-                )
+
+        def swap_halves(h0, h1):
+            count = (h1 - h0) * PAIRS
+            other = psum.tile([P, count, CHANNELS], F32, name="other", tag="bank%d" % (h0 * PAIRS))
+            nc.tensor.matmul(
+                out=other[:].rearrange("p b c -> p (b c)"),
+                lhsT=swap[:],
+                rhs=own[:, h0 * PAIRS : h1 * PAIRS, :].rearrange("p b c -> p (b c)"),
+                start=True,
+                stop=True,
+            )
             return other
 
-        def assemble(u, other, copies):
-            unit = slice(u * UNIT_BANKS, (u + 1) * UNIT_BANKS)
+        def assemble_own(h0, h1, copies):
+            group = slice(h0 * PAIRS, h1 * PAIRS)
             for d in range(2):
                 mine = slice(d * HALF_CHANNELS, (d + 1) * HALF_CHANNELS)
                 copies[d](
-                    out=final[halves[d], :, unit, d],
-                    in_=own[halves[d], unit, mine].rearrange("p b c -> p c b"),
+                    out=final[halves[d], :, group, d],
+                    in_=own[halves[d], group, mine].rearrange("p b c -> p c b"),
                 )
+
+        def assemble_other(h0, h1, other, copies):
+            group = slice(h0 * PAIRS, h1 * PAIRS)
             for d in range(2):
                 mine = slice(d * HALF_CHANNELS, (d + 1) * HALF_CHANNELS)
                 copies[d](
-                    out=final[halves[d], :, unit, 1 - d],
+                    out=final[halves[d], :, group, 1 - d],
                     in_=other[halves[d], :, mine].rearrange("p b c -> p c b"),
                 )
 
         loaded = [load_pass(s) for s in range(RAW_BUFS)]
+        both = (nc.vector.tensor_copy, nc.scalar.copy)
+        scalar_only = (nc.scalar.copy, nc.scalar.copy)
+        tiles_of = {}
         waiting = None
-        for s in range(PASSES):
+        for s, h0, h1 in UNITS:
+            if h0 == 0:
+                tiles_of[s] = pass_tiles()
             x_raw, g_raw = loaded[s]
-            for u in range(UNITS):
-                x_grp, g_grp = regroup(x_raw, g_raw, u)
-                if waiting is not None:
-                    quantise_and_multiply(*waiting)
-                waiting = (x_grp, g_grp, s, u)
-            if s + RAW_BUFS < PASSES:
+            regroup(x_raw, g_raw, tiles_of[s], h0, h1)
+            if waiting is not None:
+                quantise_and_multiply(*waiting)
+            waiting = (tiles_of[s], s, h0, h1)
+            if h1 == H and s + RAW_BUFS < PASSES:
                 loaded.append(load_pass(s + RAW_BUFS))
 
-        both = (nc.vector.tensor_copy, nc.scalar.copy)
-        other_0 = pick_and_swap(0, (nc.scalar.copy, nc.scalar.copy))
+        pick(0, 2, scalar_only)
         quantise_and_multiply(*waiting)
-        assemble(0, other_0, both)
-        other_1 = pick_and_swap(1, both)
-        assemble(1, other_1, both)
+        other_a = swap_halves(0, 2)
+        pick(2, 3, scalar_only)
+        other_b = swap_halves(2, 3)
+        pick(3, 4, both)
+        other_c = swap_halves(3, 4)
+        assemble_own(0, 2, both)
+        assemble_own(2, 3, both)
+        assemble_own(3, 4, both)
+        assemble_other(0, 2, other_a, both)
+        assemble_other(2, 3, other_b, both)
+        assemble_other(3, 4, other_c, both)
 
         out_halves = out.rearrange("f (d c) h w -> d f (c h w)", d=2)
         final_flat = final[:].rearrange("p c b e -> p (c b e)")

@@ -75,16 +75,16 @@ def tile_convdct_pa_k_kernel(tc, x_dct, k_dct, grad_out, out):
                 out=x_raw[:].rearrange("p t c h w -> p (t c h w)"),
                 in_=x_dct[rows].rearrange("(p t) c h w -> p (t c h w)", t=PACK),
             )
-            g_raw = raw.tile([P, PACK, FILTERS, H, W], BF16, name="g_raw")
+            g_raw = raw.tile([P, PACK, FILTERS, BANKS, 2], BF16, name="g_raw")
             nc.sync.dma_start(
-                out=g_raw[:].rearrange("p t f h w -> p (t f h w)"),
+                out=g_raw[:].rearrange("p t f b e -> p (t f b e)"),
                 in_=grad_out[rows].rearrange("(p t) f h w -> p (t f h w)", t=PACK),
             )
             return x_raw, g_raw
 
         def pass_tiles():
             return dict(
-                g_grp=grouped.tile([P, H, W, FILTERS, PACK], BF16, name="g_grp", align_bytes=64),
+                g_grp=grouped.tile([P, BANKS, FILTERS, 2, PACK], BF16, name="g_grp", align_bytes=64),
                 x_grp=grouped.tile([P, H, CHANNELS, W, PACK], BF16, name="x_grp", align_bytes=64),
                 g_codes=quantised.tile([P, G_COLS], U32, name="g_codes", align_bytes=64),
                 g_scales=quantised.tile([P, G_COLS], U8, name="g_scales", align_bytes=64),
@@ -94,10 +94,12 @@ def tile_convdct_pa_k_kernel(tc, x_dct, k_dct, grad_out, out):
 
         def regroup(x_raw, g_raw, tiles, h0, h1):
             rows = slice(h0, h1)
-            nc.vector.tensor_copy(
-                out=tiles["g_grp"][:, rows, :, :, :].rearrange("p h w f t -> p h f t w"),
-                in_=g_raw[:, :, :, rows, :].rearrange("p t f h w -> p h f t w"),
-            )
+            for first in range(h0, h1, 2):
+                four = slice(first * PAIRS, min(first + 2, h1) * PAIRS)
+                nc.vector.tensor_copy(
+                    out=tiles["g_grp"][:, four, :, :, :].rearrange("p b f e t -> p f t b e"),
+                    in_=g_raw[:, :, :, four, :].rearrange("p t f b e -> p f t b e"),
+                )
             nc.vector.tensor_copy(
                 out=tiles["x_grp"][:, rows, 0:X_ON_VECTOR, :, :].rearrange("p h c w t -> p h c t w"),
                 in_=x_raw[:, :, 0:X_ON_VECTOR, rows, :].rearrange("p t c h w -> p h c t w"),
@@ -110,7 +112,7 @@ def tile_convdct_pa_k_kernel(tc, x_dct, k_dct, grad_out, out):
                 )
 
         def quantise_and_multiply(tiles, s, h0, h1):
-            g_flat = tiles["g_grp"][:].rearrange("p h w f t -> p (h w f t)")
+            g_flat = tiles["g_grp"][:].rearrange("p b f e t -> p (b f e t)")
             for first, last in quantise_pieces(h0 * G_ROW, h1 * G_ROW):
                 nc.vector.quantize_mx(
                     out=tiles["g_codes"][:, first:last].bitcast(E5M2_X4),
@@ -138,60 +140,40 @@ def tile_convdct_pa_k_kernel(tc, x_dct, k_dct, grad_out, out):
                         stop=(s == PASSES - 1),
                     )
 
-        identity = consts.tile([P, P], F32, name="identity")
-        make_identity(nc, identity[:])
-        swap = consts.tile([P, P], F32, name="swap")
-        nc.vector.tensor_copy(out=swap[:, 0:FILTERS], in_=identity[:, FILTERS:P])
-        nc.vector.tensor_copy(out=swap[:, FILTERS:P], in_=identity[:, 0:FILTERS])
+        identity = consts.tile([P, FILTERS, 2], F32, name="identity")
+        make_identity(nc, identity[:].rearrange("p f j -> p (f j)"))
+        route = consts.tile([P, 2, 2, FILTERS, 2], F32, name="route")
+        nc.gpsimd.memset(route[:], 0.0)
+        for e in range(2):
+            for d in range(2):
+                nc.gpsimd.tensor_copy(out=route[:, e, d, :, d], in_=identity[:, :, e])
 
-        own = results.tile([P, BANKS, CHANNELS], F32, name="own")
+        picked = results.tile([P, BANKS, 2, CHANNELS], F32, name="picked")
         final = results.tile([P, HALF_CHANNELS, BANKS, 2], F32, name="final")
-        halves = (slice(0, FILTERS), slice(FILTERS, P))
 
-        def pick(h0, h1, copies):
+        def pick(b, copy):
+            h, q = divmod(b, PAIRS)
+            first = h * X_ROW - window_start(h)
+            row = banks[b][:, first : first + X_ROW].rearrange("p (c q e) -> p q e c", q=PAIRS, e=2)
+            copy(out=picked[:, b, :, :], in_=row[:, q, :, :])
+
+        def select(b0, b1):
+            chosen = psum.tile([P, 2, b1 - b0, HALF_CHANNELS], F32, name="chosen", tag="bank%d" % b0)
             for e in range(2):
-                for b in range(h0 * PAIRS, h1 * PAIRS):
-                    h, q = divmod(b, PAIRS)
-                    first = h * X_ROW - window_start(h)
-                    row = banks[b][halves[e], first : first + X_ROW]
-                    copies[e](
-                        out=own[halves[e], b, :],
-                        in_=row.rearrange("p (c w) -> p c w", w=W)[:, :, 2 * q + e],
+                for d in range(2):
+                    nc.tensor.matmul(
+                        out=chosen[:, e, :, :],
+                        lhsT=route[:, e, d, :, :].rearrange("p f j -> p (f j)"),
+                        rhs=picked[:, b0:b1, e, d * HALF_CHANNELS : (d + 1) * HALF_CHANNELS],
+                        start=(d == 0),
+                        stop=(d == 1),
                     )
+            return chosen
 
-        def swap_halves(h0, h1):
-            count = (h1 - h0) * PAIRS
-            other = psum.tile([P, count, CHANNELS], F32, name="other", tag="bank%d" % (h0 * PAIRS))
-            nc.tensor.matmul(
-                out=other[:].rearrange("p b c -> p (b c)"),
-                lhsT=swap[:],
-                rhs=own[:, h0 * PAIRS : h1 * PAIRS, :].rearrange("p b c -> p (b c)"),
-                start=True,
-                stop=True,
-            )
-            return other
-
-        def assemble_own(h0, h1, copies):
-            group = slice(h0 * PAIRS, h1 * PAIRS)
-            for d in range(2):
-                mine = slice(d * HALF_CHANNELS, (d + 1) * HALF_CHANNELS)
-                copies[d](
-                    out=final[halves[d], :, group, d],
-                    in_=own[halves[d], group, mine].rearrange("p b c -> p c b"),
-                )
-
-        def assemble_other(h0, h1, other, copies):
-            group = slice(h0 * PAIRS, h1 * PAIRS)
-            for d in range(2):
-                mine = slice(d * HALF_CHANNELS, (d + 1) * HALF_CHANNELS)
-                copies[d](
-                    out=final[halves[d], :, group, 1 - d],
-                    in_=other[halves[d], :, mine].rearrange("p b c -> p c b"),
-                )
+        def assemble(b0, b1, chosen, copy):
+            copy(out=final[:, :, b0:b1, :], in_=chosen[:].rearrange("p e b c -> p c b e"))
 
         loaded = [load_pass(s) for s in range(RAW_BUFS)]
-        both = (nc.vector.tensor_copy, nc.scalar.copy)
-        scalar_only = (nc.scalar.copy, nc.scalar.copy)
         tiles_of = {}
         waiting = None
         for s, h0, h1 in UNITS:
@@ -205,21 +187,21 @@ def tile_convdct_pa_k_kernel(tc, x_dct, k_dct, grad_out, out):
             if h1 == H and s + RAW_BUFS < PASSES:
                 loaded.append(load_pass(s + RAW_BUFS))
 
-        pick(0, 2, scalar_only)
+        for b in range(0, 4):
+            pick(b, nc.scalar.copy)
         quantise_and_multiply(*waiting)
-        other_a = swap_halves(0, 2)
-        pick(2, 3, scalar_only)
-        other_b = swap_halves(2, 3)
-        pick(3, 4, both)
-        other_c = swap_halves(3, 4)
-        assemble_own(0, 2, both)
-        assemble_own(2, 3, both)
-        assemble_own(3, 4, both)
-        assemble_other(0, 2, other_a, both)
-        assemble_other(2, 3, other_b, both)
-        assemble_other(3, 4, other_c, both)
+        chosen_a = select(0, 4)
+        for b in range(4, 6):
+            pick(b, nc.scalar.copy)
+        chosen_b = select(4, 6)
+        pick(6, nc.vector.tensor_copy)
+        pick(7, nc.scalar.copy)
+        chosen_c = select(6, 8)
+        assemble(0, 4, chosen_a, nc.vector.tensor_copy)
+        assemble(4, 6, chosen_b, nc.scalar.copy)
+        assemble(6, 8, chosen_c, nc.vector.tensor_copy)
 
-        out_halves = out.rearrange("f (d c) h w -> d f (c h w)", d=2)
-        final_flat = final[:].rearrange("p c b e -> p (c b e)")
-        nc.sync.dma_start(out=out_halves[0], in_=final_flat[halves[0]])
-        nc.scalar.dma_start(out=out_halves[1], in_=final_flat[halves[1]])
+        nc.sync.dma_start(
+            out=out.rearrange("f (d c) h w -> (f d) (c h w)", d=2),
+            in_=final[:].rearrange("p c b e -> p (c b e)"),
+        )

@@ -29,7 +29,8 @@ N_MOVING = 512
 MAX_QUANT_COLS = 1024
 HALF_CHANNELS = CHANNELS // 2
 
-X_ON_VECTOR = 4
+X_ON_SCALAR = 6
+X_ON_VECTOR = CHANNELS - X_ON_SCALAR
 
 RAW_BUFS = 4
 PASS_BUFS = 3
@@ -94,12 +95,6 @@ def tile_convdct_pa_k_kernel(tc, x_dct, k_dct, grad_out, out):
 
         def regroup(x_raw, g_raw, tiles, h0, h1):
             rows = slice(h0, h1)
-            for first in range(h0, h1, 2):
-                four = slice(first * PAIRS, min(first + 2, h1) * PAIRS)
-                nc.vector.tensor_copy(
-                    out=tiles["g_grp"][:, four, :, :, :].rearrange("p b f e t -> p f t b e"),
-                    in_=g_raw[:, :, :, four, :].rearrange("p t f b e -> p f t b e"),
-                )
             nc.vector.tensor_copy(
                 out=tiles["x_grp"][:, rows, 0:X_ON_VECTOR, :, :].rearrange("p h c w t -> p h c t w"),
                 in_=x_raw[:, :, 0:X_ON_VECTOR, rows, :].rearrange("p t c h w -> p h c t w"),
@@ -110,21 +105,27 @@ def tile_convdct_pa_k_kernel(tc, x_dct, k_dct, grad_out, out):
                     out=tiles["x_grp"][:, two, X_ON_VECTOR:, :, :].rearrange("p h c w t -> p c t h w"),
                     in_=x_raw[:, :, X_ON_VECTOR:, two, :].rearrange("p t c h w -> p c t h w"),
                 )
+            for first in range(h0, h1, 2):
+                four = slice(first * PAIRS, min(first + 2, h1) * PAIRS)
+                nc.scalar.copy(
+                    out=tiles["g_grp"][:, four, :, :, :].rearrange("p b f e t -> p f t b e"),
+                    in_=g_raw[:, :, :, four, :].rearrange("p t f b e -> p f t b e"),
+                )
 
         def quantise_and_multiply(tiles, s, h0, h1):
-            g_flat = tiles["g_grp"][:].rearrange("p b f e t -> p (b f e t)")
-            for first, last in quantise_pieces(h0 * G_ROW, h1 * G_ROW):
-                nc.vector.quantize_mx(
-                    out=tiles["g_codes"][:, first:last].bitcast(E5M2_X4),
-                    scales=tiles["g_scales"][:, first:last],
-                    in_=g_flat[:, first * PACK : last * PACK],
-                )
             x_flat = tiles["x_grp"][:].rearrange("p h c w t -> p (h c w t)")
             for first, last in quantise_pieces(h0 * X_ROW, h1 * X_ROW):
                 nc.vector.quantize_mx(
                     out=tiles["x_codes"][:, first:last].bitcast(E4M3_X4),
                     scales=tiles["x_scales"][:, first:last],
                     in_=x_flat[:, first * PACK : last * PACK],
+                )
+            g_flat = tiles["g_grp"][:].rearrange("p b f e t -> p (b f e t)")
+            for first, last in quantise_pieces(h0 * G_ROW, h1 * G_ROW):
+                nc.vector.quantize_mx(
+                    out=tiles["g_codes"][:, first:last].bitcast(E5M2_X4),
+                    scales=tiles["g_scales"][:, first:last],
+                    in_=g_flat[:, first * PACK : last * PACK],
                 )
             for h in range(h0, h1):
                 window = slice(window_start(h), window_start(h) + N_MOVING)

@@ -29,7 +29,7 @@ N_MOVING = 512
 MAX_QUANT_COLS = 1024
 HALF_CHANNELS = CHANNELS // 2
 
-X_ON_SCALAR = 6
+X_ON_SCALAR = 8
 X_ON_VECTOR = CHANNELS - X_ON_SCALAR
 
 RAW_BUFS = 4

@@ -29,8 +29,7 @@ N_MOVING = 512
 MAX_QUANT_COLS = 1024
 HALF_CHANNELS = CHANNELS // 2
 
-X_ON_SCALAR = 8
-X_ON_VECTOR = CHANNELS - X_ON_SCALAR
+X_ON_SCALAR = (6, 8)
 
 RAW_BUFS = 4
 PASS_BUFS = 3
@@ -93,17 +92,18 @@ def tile_convdct_pa_k_kernel(tc, x_dct, k_dct, grad_out, out):
                 x_scales=quantised.tile([P, X_COLS], U8, name="x_scales", align_bytes=64),
             )
 
-        def regroup(x_raw, g_raw, tiles, h0, h1):
+        def regroup(s, x_raw, g_raw, tiles, h0, h1):
             rows = slice(h0, h1)
+            on_vector = CHANNELS - X_ON_SCALAR[s % 2]
             nc.vector.tensor_copy(
-                out=tiles["x_grp"][:, rows, 0:X_ON_VECTOR, :, :].rearrange("p h c w t -> p h c t w"),
-                in_=x_raw[:, :, 0:X_ON_VECTOR, rows, :].rearrange("p t c h w -> p h c t w"),
+                out=tiles["x_grp"][:, rows, 0:on_vector, :, :].rearrange("p h c w t -> p h c t w"),
+                in_=x_raw[:, :, 0:on_vector, rows, :].rearrange("p t c h w -> p h c t w"),
             )
             for first in range(h0, h1, 2):
                 two = slice(first, min(first + 2, h1))
                 nc.scalar.copy(
-                    out=tiles["x_grp"][:, two, X_ON_VECTOR:, :, :].rearrange("p h c w t -> p c t h w"),
-                    in_=x_raw[:, :, X_ON_VECTOR:, two, :].rearrange("p t c h w -> p c t h w"),
+                    out=tiles["x_grp"][:, two, on_vector:, :, :].rearrange("p h c w t -> p c t h w"),
+                    in_=x_raw[:, :, on_vector:, two, :].rearrange("p t c h w -> p c t h w"),
                 )
             for first in range(h0, h1, 2):
                 four = slice(first * PAIRS, min(first + 2, h1) * PAIRS)
@@ -112,7 +112,7 @@ def tile_convdct_pa_k_kernel(tc, x_dct, k_dct, grad_out, out):
                     in_=g_raw[:, :, :, four, :].rearrange("p t f b e -> p f t b e"),
                 )
 
-        def quantise_and_multiply(tiles, s, h0, h1):
+        def quantise_x(tiles, s, h0, h1):
             x_flat = tiles["x_grp"][:].rearrange("p h c w t -> p (h c w t)")
             for first, last in quantise_pieces(h0 * X_ROW, h1 * X_ROW):
                 nc.vector.quantize_mx(
@@ -120,6 +120,8 @@ def tile_convdct_pa_k_kernel(tc, x_dct, k_dct, grad_out, out):
                     scales=tiles["x_scales"][:, first:last],
                     in_=x_flat[:, first * PACK : last * PACK],
                 )
+
+        def quantise_g_and_multiply(tiles, s, h0, h1):
             g_flat = tiles["g_grp"][:].rearrange("p b f e t -> p (b f e t)")
             for first, last in quantise_pieces(h0 * G_ROW, h1 * G_ROW):
                 nc.vector.quantize_mx(
@@ -181,16 +183,17 @@ def tile_convdct_pa_k_kernel(tc, x_dct, k_dct, grad_out, out):
             if h0 == 0:
                 tiles_of[s] = pass_tiles()
             x_raw, g_raw = loaded[s]
-            regroup(x_raw, g_raw, tiles_of[s], h0, h1)
+            regroup(s, x_raw, g_raw, tiles_of[s], h0, h1)
             if waiting is not None:
-                quantise_and_multiply(*waiting)
+                quantise_g_and_multiply(*waiting)
             waiting = (tiles_of[s], s, h0, h1)
+            quantise_x(*waiting)
             if h1 == H and s + RAW_BUFS < PASSES:
                 loaded.append(load_pass(s + RAW_BUFS))
 
         for b in range(0, 4):
             pick(b, nc.scalar.copy)
-        quantise_and_multiply(*waiting)
+        quantise_g_and_multiply(*waiting)
         chosen_a = select(0, 4)
         for b in range(4, 6):
             pick(b, nc.scalar.copy)

from contextlib import ExitStack

import concourse.mybir as mybir
from concourse.masks import make_identity

BF16 = mybir.dt.bfloat16
F32 = mybir.dt.float32
U32 = mybir.dt.uint32
U8 = mybir.dt.uint8
E4M3_X4 = mybir.dt.float8_e4m3fn_x4
E5M2_X4 = mybir.dt.float8_e5m2_x4

IMAGES, CHANNELS, FILTERS = 8192, 80, 64
P = 128
PACK = 4
K_PASS = P * PACK
PASSES = IMAGES // K_PASS
H = 4
W = 4
PAIRS = W // 2
BANKS = H * PAIRS

G_PAIR = 2 * FILTERS
G_ROW = W * FILTERS
X_ROW = W * CHANNELS
G_COLS = H * G_ROW
X_COLS = H * X_ROW
N_MOVING = 512
MAX_QUANT_COLS = 1024
HALF_CHANNELS = CHANNELS // 2

X_ON_SCALAR = (6, 8)

RAW_BUFS = 4
PASS_BUFS = 3

FLOPS = 2 * 16 * FILTERS * CHANNELS * IMAGES
BYTES = 2 * IMAGES * 16 * (CHANNELS + FILTERS) + 4 * 16 * FILTERS * CHANNELS

UNITS = [(s, 0, H) for s in range(PASSES - 1)] + [(PASSES - 1, 0, 2), (PASSES - 1, 2, 3), (PASSES - 1, 3, 4)]


def window_start(h):
    return 0 if h == 0 else (h + 1) * X_ROW - N_MOVING


def quantise_pieces(first, last):
    pieces = []
    while first < last:
        width = MAX_QUANT_COLS
        while width > last - first:
            width //= 2
        pieces.append((first, first + width))
        first += width
    return pieces


def tile_convdct_pa_k_kernel(tc, x_dct, k_dct, grad_out, out):
    nc = tc.nc
    with ExitStack() as ctx:
        ctx.enter_context(tc.manual_schedule())
        consts = ctx.enter_context(tc.tile_pool(name="consts", bufs=1))
        raw = ctx.enter_context(tc.tile_pool(name="raw", bufs=RAW_BUFS))
        grouped = ctx.enter_context(tc.tile_pool(name="grouped", bufs=PASS_BUFS))
        quantised = ctx.enter_context(tc.tile_pool(name="quantised", bufs=PASS_BUFS))
        results = ctx.enter_context(tc.tile_pool(name="results", bufs=1))
        psum = ctx.enter_context(tc.psum_pool(name="psum", bufs=1))

        banks = [psum.tile([P, N_MOVING], F32, name="bank%d" % b) for b in range(BANKS)]

        def load_pass(s):
            rows = slice(s * K_PASS, (s + 1) * K_PASS)
            x_raw = raw.tile([P, PACK, CHANNELS, H, W], BF16, name="x_raw")
            nc.sync.dma_start(
                out=x_raw[:].rearrange("p t c h w -> p (t c h w)"),
                in_=x_dct[rows].rearrange("(p t) c h w -> p (t c h w)", t=PACK),
            )
            g_raw = raw.tile([P, PACK, FILTERS, BANKS, 2], BF16, name="g_raw")
            nc.sync.dma_start(
                out=g_raw[:].rearrange("p t f b e -> p (t f b e)"),
                in_=grad_out[rows].rearrange("(p t) f h w -> p (t f h w)", t=PACK),
            )
            return x_raw, g_raw

        def pass_tiles():
            return dict(
                g_grp=grouped.tile([P, BANKS, FILTERS, 2, PACK], BF16, name="g_grp", align_bytes=64),
                x_grp=grouped.tile([P, H, CHANNELS, W, PACK], BF16, name="x_grp", align_bytes=64),
                g_codes=quantised.tile([P, G_COLS], U32, name="g_codes", align_bytes=64),
                g_scales=quantised.tile([P, G_COLS], U8, name="g_scales", align_bytes=64),
                x_codes=quantised.tile([P, X_COLS], U32, name="x_codes", align_bytes=64),
                x_scales=quantised.tile([P, X_COLS], U8, name="x_scales", align_bytes=64),
            )

        def regroup(s, x_raw, g_raw, tiles, h0, h1):
            rows = slice(h0, h1)
            on_vector = CHANNELS - X_ON_SCALAR[s % 2]
            nc.vector.tensor_copy(
                out=tiles["x_grp"][:, rows, 0:on_vector, :, :].rearrange("p h c w t -> p h c t w"),
                in_=x_raw[:, :, 0:on_vector, rows, :].rearrange("p t c h w -> p h c t w"),
            )
            for first in range(h0, h1, 2):
                two = slice(first, min(first + 2, h1))
                nc.scalar.copy(
                    out=tiles["x_grp"][:, two, on_vector:, :, :].rearrange("p h c w t -> p c t h w"),
                    in_=x_raw[:, :, on_vector:, two, :].rearrange("p t c h w -> p c t h w"),
                )
            for first in range(h0, h1, 2):
                four = slice(first * PAIRS, min(first + 2, h1) * PAIRS)
                nc.scalar.copy(
                    out=tiles["g_grp"][:, four, :, :, :].rearrange("p b f e t -> p f t b e"),
                    in_=g_raw[:, :, :, four, :].rearrange("p t f b e -> p f t b e"),
                )

        def quantise_x(tiles, s, h0, h1):
            x_flat = tiles["x_grp"][:].rearrange("p h c w t -> p (h c w t)")
            for first, last in quantise_pieces(h0 * X_ROW, h1 * X_ROW):
                nc.vector.quantize_mx(
                    out=tiles["x_codes"][:, first:last].bitcast(E4M3_X4),
                    scales=tiles["x_scales"][:, first:last],
                    in_=x_flat[:, first * PACK : last * PACK],
                )

        def quantise_g_and_multiply(tiles, s, h0, h1):
            g_flat = tiles["g_grp"][:].rearrange("p b f e t -> p (b f e t)")
            for first, last in quantise_pieces(h0 * G_ROW, h1 * G_ROW):
                nc.vector.quantize_mx(
                    out=tiles["g_codes"][:, first:last].bitcast(E5M2_X4),
                    scales=tiles["g_scales"][:, first:last],
                    in_=g_flat[:, first * PACK : last * PACK],
                )
            for h in range(h0, h1):
                window = slice(window_start(h), window_start(h) + N_MOVING)
                for q in range(PAIRS):
                    pair = slice((h * PAIRS + q) * G_PAIR, (h * PAIRS + q + 1) * G_PAIR)
                    nc.tensor.matmul_mx(
                        out=banks[h * PAIRS + q][:],
                        lhsT=tiles["g_codes"][:, pair].bitcast(E5M2_X4),
                        lhsT_scale=tiles["g_scales"][:, pair],
                        rhs=tiles["x_codes"][:, window].bitcast(E4M3_X4),
                        rhs_scale=tiles["x_scales"][:, window],
                        start=(s == 0),
                        stop=(s == PASSES - 1),
                    )

        identity = consts.tile([P, FILTERS, 2], F32, name="identity")
        make_identity(nc, identity[:].rearrange("p f j -> p (f j)"))
        route = consts.tile([P, 2, 2, FILTERS, 2], F32, name="route")
        nc.gpsimd.memset(route[:], 0.0)
        for e in range(2):
            for d in range(2):
                nc.gpsimd.tensor_copy(out=route[:, e, d, :, d], in_=identity[:, :, e])

        picked = results.tile([P, BANKS, 2, CHANNELS], F32, name="picked")
        final = results.tile([P, HALF_CHANNELS, BANKS, 2], F32, name="final")

        def pick(b, copy):
            h, q = divmod(b, PAIRS)
            first = h * X_ROW - window_start(h)
            row = banks[b][:, first : first + X_ROW].rearrange("p (c q e) -> p q e c", q=PAIRS, e=2)
            copy(out=picked[:, b, :, :], in_=row[:, q, :, :])

        def select(b0, b1):
            chosen = psum.tile([P, 2, b1 - b0, HALF_CHANNELS], F32, name="chosen", tag="bank%d" % b0)
            for e in range(2):
                for d in range(2):
                    nc.tensor.matmul(
                        out=chosen[:, e, :, :],
                        lhsT=route[:, e, d, :, :].rearrange("p f j -> p (f j)"),
                        rhs=picked[:, b0:b1, e, d * HALF_CHANNELS : (d + 1) * HALF_CHANNELS],
                        start=(d == 0),
                        stop=(d == 1),
                    )
            return chosen

        def assemble(b0, b1, chosen, copy):
            copy(out=final[:, :, b0:b1, :], in_=chosen[:].rearrange("p e b c -> p c b e"))

        loaded = [load_pass(s) for s in range(RAW_BUFS)]
        tiles_of = {}
        waiting = None
        for s, h0, h1 in UNITS:
            if h0 == 0:
                tiles_of[s] = pass_tiles()
            x_raw, g_raw = loaded[s]
            regroup(s, x_raw, g_raw, tiles_of[s], h0, h1)
            if waiting is not None:
                quantise_g_and_multiply(*waiting)
            waiting = (tiles_of[s], s, h0, h1)
            quantise_x(*waiting)
            if h1 == H and s + RAW_BUFS < PASSES:
                loaded.append(load_pass(s + RAW_BUFS))

        for b in range(0, 4):
            pick(b, nc.scalar.copy)
        quantise_g_and_multiply(*waiting)
        chosen_a = select(0, 4)
        for b in range(4, 6):
            pick(b, nc.scalar.copy)
        chosen_b = select(4, 6)
        pick(6, nc.vector.tensor_copy)
        pick(7, nc.scalar.copy)
        chosen_c = select(6, 8)
        assemble(0, 4, chosen_a, nc.vector.tensor_copy)
        assemble(4, 6, chosen_b, nc.scalar.copy)
        assemble(6, 8, chosen_c, nc.vector.tensor_copy)

        nc.sync.dma_start(
            out=out.rearrange("f (d c) h w -> (f d) (c h w)", d=2),
            in_=final[:].rearrange("p c b e -> p (c b e)"),
        )
